import numpy as np
import ml_dtypes


def mxq(x, axis, fmt="e4m3"):
    dtype, down = {"e4m3": (ml_dtypes.float8_e4m3fn, 7), "e5m2": (ml_dtypes.float8_e5m2, 14)}[fmt]
    v = np.moveaxis(np.asarray(x, np.float32).astype(ml_dtypes.bfloat16).astype(np.float64), axis, -1)
    blocks = v.reshape(v.shape[:-1] + (-1, 32))
    amax = np.abs(blocks).max(-1, keepdims=True)
    byte = np.maximum(np.where(amax > 0, np.frexp(amax)[1] - 1 + 127, 0) - down, 1)
    scale = np.exp2(byte - 127.0)
    codes = (blocks / scale).astype(np.float32).astype(dtype).astype(np.float64)
    return np.moveaxis((codes * scale).reshape(v.shape), -1, axis)


WIDE = False


def mx_kscale(k):
    if not WIDE:
        return np.ones(k)
    levels = np.array([10, -10, 5, -5, 0])
    if k % 512:
        return np.exp2(np.random.permutation(np.resize(levels, k // 32))).repeat(32)
    a = np.empty((k // 512, 16))
    for p in range(k // 512):
        a[p, :8] = np.random.permutation(np.resize(levels, 8))
        for g in range(8):
            far = levels[np.abs(levels - a[p, g]) >= 10]
            a[p, g + 8] = far[np.random.randint(len(far))]
    return np.exp2(a.ravel()).repeat(32)


BF16 = ml_dtypes.bfloat16


def bf(x):
    return np.asarray(x, np.float32).astype(BF16)


def f64(x):
    return np.asarray(x).astype(np.float64)


E2M1 = np.array([0.0, 0.5, 1.0, 1.5, 2.0, 3.0, 4.0, 6.0, -0.0, -0.5, -1.0, -1.5, -2.0, -3.0, -4.0, -6.0])


def pack_weight(w, fmt):
    k, n = w.shape
    w = f64(bf(w)).reshape(k // 32, 32, n)
    amax = np.abs(w).max(1)
    if fmt == "e4m3":
        byte = np.frexp(amax)[1] - 1 + 127 - 7
    else:
        mant, ex = np.frexp(amax / 6.0)
        byte = np.where(mant > 0.5, ex, ex - 1) + 127
    byte = np.clip(np.where(amax > 0, byte, 1), 1, 254)
    scaled = (w * np.exp2(127.0 - byte)[:, None, :]).reshape(k, n).astype(np.float32)
    by_word = np.ascontiguousarray(scaled.reshape(k // 512, 128, 4, n).transpose(0, 1, 3, 2))
    if fmt == "e4m3":
        words = by_word.astype(ml_dtypes.float8_e4m3fn).view(np.uint8)
    else:
        c = by_word.astype(ml_dtypes.float4_e2m1fn).view(np.uint8) & 0xF
        words = c[..., 0::2] | (c[..., 1::2] << 4)
    return np.ascontiguousarray(words), np.ascontiguousarray(byte.astype(np.uint8).reshape(k // 512, 16, n))


def unpack_weight(words, scales, fmt):
    g, p, n, _ = words.shape
    if fmt == "e4m3":
        vals = np.ascontiguousarray(words).view(ml_dtypes.float8_e4m3fn).astype(np.float64)
    else:
        nib = np.empty((g, p, n, 4), np.uint8)
        nib[..., 0::2] = words & 0xF
        nib[..., 1::2] = words >> 4
        vals = E2M1[nib]
    vals = vals * np.repeat(np.exp2(scales.astype(np.float64) - 127.0), 8, axis=1)[..., None]
    return vals.transpose(0, 1, 3, 2).reshape(g * 512, n)
def pack4(w):
    words, scales = pack_weight(w, "e2m1")
    return words.reshape(words.shape[0], 128, -1), scales


def unpack4(words, scales):
    return unpack_weight(words.reshape(words.shape[0], 128, -1, 2), scales, "e2m1")


B, DIN, H0, H1, L, C, K = 1024, 1024, 2048, 1024, 512, 64, 64
BETA = 10.0


def logsumexp(a):
    m = a.max(-1, keepdims=True)
    return (m + np.log(np.exp(a - m).sum(-1, keepdims=True)))[..., 0]


def draw0():
    s, t = mx_kscale(H1), mx_kscale(L)
    h_enc = bf(np.maximum(np.random.standard_normal((B, H1)), 0.0) * s)
    words, scales = pack4(np.random.standard_normal((H1, L)) * np.sqrt(2.0 / H1) / s[:, None] * t)
    return {"h_enc": h_enc,
            "enc_w2_words": words,
            "enc_w2_scales": scales,
            "enc_b2": bf(np.random.standard_normal(L) * 0.1 * t),
            "clus_w": bf(np.random.standard_normal((C, K, L)) * 0.3 / np.sqrt(L) / t),
            "clus_b": bf(np.random.standard_normal((C, K)) * 0.1)}


def core(h_enc, enc_w2_words, enc_w2_scales, enc_b2, clus_w, clus_b):
    z = (mxq(f64(h_enc), 1, "e4m3") @ unpack4(enc_w2_words, enc_w2_scales)) + f64(enc_b2)
    wq = mxq(f64(clus_w), 2, "e4m3")
    scores = (mxq(z, 1, "e4m3") @ wq.reshape(C * K, L).T).reshape(B, C, K) + f64(clus_b)
    conf = -logsumexp(-BETA * scores)
    return z, conf


def e4m3fn_bytes(y):
    return np.clip(np.asarray(y, np.float64), -448.0, 448.0).astype(np.float32).astype(ml_dtypes.float8_e4m3fn).view(np.uint8)


def e4m3fn_values(b):
    return np.asarray(b, np.uint8).view(ml_dtypes.float8_e4m3fn).astype(np.float64)


def setup_inputs():
    d = draw0()
    x0 = np.asarray(d['clus_w']).astype(np.float64)
    s = (np.max(np.abs(x0), axis=(0, 1), keepdims=True) / 448.0).astype(np.float32)
    out = {}
    for k, v in d.items():
        if k == 'clus_w':
            out['clus_w_bytes'] = e4m3fn_bytes(x0 / s.astype(np.float64))
            out['clus_w_scale'] = s
        else:
            out[k] = v
    return out


def reference(h_enc, enc_w2_words, enc_w2_scales, enc_b2, clus_w_bytes, clus_w_scale, clus_b):
    return core(h_enc, enc_w2_words, enc_w2_scales, enc_b2, e4m3fn_values(clus_w_bytes) * clus_w_scale.astype(np.float64), clus_b)

@@ -1,0 +1,354 @@
+from contextlib import ExitStack
+
+import concourse.mybir as mybir
+from concourse.masks import make_identity
+
+B, DIN, L, C, K = 1024, 1024, 512, 64, 64
+FLOPS = 2 * B * DIN * L + 2 * B * L * C * K
+
+P = 128
+BT = B // P
+CK = C * K
+CHUNK = 512
+NCH = CK // CHUNK
+MODS = CHUNK // K
+
+F32 = mybir.dt.float32
+BF16 = mybir.dt.bfloat16
+U32 = mybir.dt.uint32
+I32 = mybir.dt.int32
+U8 = mybir.dt.uint8
+E4 = mybir.dt.float8_e4m3fn
+FP8X4 = mybir.dt.float8_e4m3fn_x4
+FP4X4 = mybir.dt.float4_e2m1fn_x4
+ALU = mybir.AluOpType
+ACT = mybir.ActivationFunctionType
+AX = mybir.AxisListType
+
+PROD = "vggggggg"
+SHIFT = frozenset()
+
+
+def tile_ace_pa_w4_kernel(tc, h_enc, w_words, w_scales, enc_b2, cw_bytes, cw_scale, clus_b, out_z, out_conf):
+    nc = tc.nc
+    with ExitStack() as ctx:
+        keep = ctx.enter_context(tc.tile_pool(name="keep", bufs=1))
+        work = ctx.enter_context(tc.tile_pool(name="work", bufs=3))
+        psum = ctx.enter_context(tc.psum_pool(name="psum", bufs=1))
+        ctx.enter_context(tc.manual_schedule())
+
+        ident = keep.tile([P, P], F32, name="ident")
+        h_in = keep.tile([P, BT, DIN], BF16, name="h_in", align_bytes=64)
+        wq = keep.tile([P, 2, 2 * L], U8, name="wq", align_bytes=64)
+        wqs = keep.tile([P, 2, L], U8, name="wqs", align_bytes=64)
+        b2 = keep.tile([P, L], BF16, name="b2", align_bytes=64)
+        scale = keep.tile([P, L], F32, name="scale", align_bytes=64)
+        cwb = keep.tile([P, NCH, 2, 2 * L], U8, name="cwb", align_bytes=64)
+        cb = keep.tile([P, CK], BF16, name="cb", align_bytes=64)
+        cb10 = keep.tile([P, CK], F32, name="cb10", align_bytes=64)
+        zc = keep.tile([P, B], U32, name="zc", align_bytes=64)
+        zs = keep.tile([P, B], U8, name="zs", align_bytes=64)
+        mn = keep.tile([P, BT, C], F32, name="mn", align_bytes=64)
+        sums = keep.tile([P, BT, C], F32, name="sums", align_bytes=64)
+        dummy = keep.tile([P, 8], F32, name="dummy")
+        dummy2 = keep.tile([P, 8], F32, name="dummy2")
+
+        def load_h(i):
+            nc.sync.dma_start(out=h_in[:, i, :], in_=h_enc[P * i : P * (i + 1), :])
+
+        cw_rows = cw_bytes.rearrange("m h d -> (m h) d").rearrange("(c a r j) d -> c r a (j d)", a=2, r=P, j=2)
+
+        def load_w(c):
+            nc.sync.dma_start(out=cwb[:, c, :, :], in_=cw_rows[c])
+
+        cb_row = clus_b.rearrange("c k -> (c k)")
+
+        def load_cb(s, e):
+            nc.sync.dma_start(out=cb[:, s:e], in_=cb_row[s:e].partition_broadcast(P))
+
+        nc.gpsimd.memset(wqs[:].rearrange("p g n -> p (g n)").bitcast(I32), 0)
+        nc.gpsimd.memset(dummy[:], 0.0)
+        make_identity(nc, ident[:])
+        nc.scalar.activation(out=dummy2[:], in_=dummy[:], func=ACT.Exp)
+
+        load_h(0)
+        load_h(1)
+        nc.sync.dma_start(out=wq[:], in_=w_words.rearrange("g p x -> p g x"))
+        for q in range(4):
+            nc.sync.dma_start(
+                out=wqs[32 * q : 32 * q + 4, :, :].bitcast(I32),
+                in_=w_scales[:, 4 * q : 4 * q + 4, :].rearrange("g r n -> r g n").bitcast(I32),
+            )
+        nc.sync.dma_start(out=scale[:], in_=cw_scale.rearrange("a b d -> (a b d)").partition_broadcast(P))
+        load_w(0)
+        load_h(2)
+        load_h(3)
+        nc.sync.dma_start(out=b2[:], in_=enc_b2.partition_broadcast(P))
+        load_cb(0, 512)
+        load_w(1)
+        for i in range(4, BT):
+            load_h(i)
+        load_cb(512, 2048)
+        load_w(2)
+        load_w(3)
+        load_cb(2048, 4096)
+        for c in range(4, NCH):
+            load_w(c)
+
+        def bank_tile(tag, bufs):
+            t = psum.tile([P, 4, P], F32, name=tag, tag=tag, bufs=bufs)
+            return t
+
+        hg = {}
+        hc = {}
+        hs = {}
+        zf = {}
+        zb = {}
+        zg = {}
+        prod = {}
+        wg = {}
+        wc = {}
+        ws = {}
+
+        def h_transpose(i):
+            words = h_in[:, i, :].bitcast(F32)
+            t = bank_tile("tr", 3)
+            for g in range(2):
+                for u in range(2):
+                    nc.tensor.transpose(t[:, 2 * g + u, :], words[:, 256 * g + u : 256 * (g + 1) : 2], ident[:])
+            hg[i] = work.tile([P, 4 * 256], BF16, name="hg", tag="hg", bufs=3, align_bytes=64)
+            nc.scalar.copy(
+                out=hg[i][:].bitcast(F32).rearrange("p (g b u) -> p g b u", g=2, u=2),
+                in_=t[:].rearrange("p (g u) b -> p g b u", u=2),
+            )
+
+        def h_quant(i):
+            hc[i] = work.tile([P, 256], U32, name="hc", tag="hc", bufs=4, align_bytes=64)
+            hs[i] = work.tile([P, 256], U8, name="hs", tag="hs", bufs=4, align_bytes=64)
+            nc.vector.quantize_mx(out=hc[i][:].bitcast(FP8X4), scales=hs[i][:], in_=hg[i][:])
+
+        zps = {}
+
+        def z_matmul(i):
+            zps[i] = psum.tile([P, 512], F32, name="mm", tag="mm", bufs=5)
+            for g in range(2):
+                nc.tensor.matmul_mx(
+                    out=zps[i][:],
+                    lhsT=hc[i][:, P * g : P * (g + 1)].bitcast(FP8X4),
+                    lhsT_scale=hs[i][:, P * g : P * (g + 1)],
+                    rhs=wq[:, g, :].bitcast(FP4X4),
+                    rhs_scale=wqs[:, g, :],
+                    start=(g == 0),
+                    stop=(g == 1),
+                )
+
+        def z_add(i):
+            zf[i] = work.tile([P, L], F32, name="zf", tag="zf", bufs=4, align_bytes=64)
+            nc.vector.tensor_tensor(out=zf[i][:], in0=zps[i][:], in1=b2[:], op=ALU.add)
+            nc.sync.dma_start(out=out_z[P * i : P * (i + 1), :], in_=zf[i][:])
+
+        def z_round(i):
+            zb[i] = work.tile([P, L], BF16, name="zb", tag="zb", bufs=4, align_bytes=64)
+            nc.vector.tensor_copy(out=zb[i][:], in_=zf[i][:])
+
+        def z_transpose(j):
+            t = bank_tile("tr", 3)
+            for a in range(2):
+                words = zb[2 * j + a][:].bitcast(F32)
+                for u in range(2):
+                    nc.tensor.transpose(t[:, 2 * a + u, :], words[:, u::2], ident[:])
+            zg[j] = work.tile([P, 4 * 256], BF16, name="zg", tag="zg", bufs=2, align_bytes=64)
+            nc.scalar.copy(
+                out=zg[j][:].bitcast(F32).rearrange("p (a b u) -> p a b u", a=2, u=2),
+                in_=t[:].rearrange("p (a u) b -> p a b u", u=2),
+            )
+
+        def z_quant(j):
+            cols = slice(256 * j, 256 * (j + 1))
+            nc.vector.quantize_mx(out=zc[:, cols].bitcast(FP8X4), scales=zs[:, cols], in_=zg[j][:])
+
+        def w_prod(c, a, j):
+            if j == 0:
+                prod[c, a] = work.tile([P, 2, L], BF16, name="prod", tag="prod", bufs=6, align_bytes=64)
+            src = cwb[:, c, a, L * j : L * (j + 1)].bitcast(E4)
+            dst = prod[c, a][:, j, :]
+            if PROD[c] == "v":
+                nc.vector.tensor_tensor(out=dst, in0=src, in1=scale[:], op=ALU.mult)
+            else:
+                wide = work.tile([P, L], BF16, name="wide", tag="wide", bufs=4, align_bytes=64)
+                if PROD[c] == "g":
+                    nc.gpsimd.tensor_copy(out=wide[:], in_=src)
+                elif PROD[c] == "m":
+                    nc.vector.tensor_copy(out=wide[:], in_=src)
+                nc.gpsimd.tensor_tensor(out=dst, in0=wide[:], in1=scale[:], op=ALU.mult)
+
+        def w_transpose(c, a):
+            if a == 0:
+                wg[c] = work.tile([P, 4 * CHUNK], BF16, name="wg", tag="wg", bufs=2, align_bytes=64)
+            t = bank_tile("tr", 3)
+            for j in range(2):
+                words = prod[c, a][:, j, :].bitcast(F32)
+                for u in range(2):
+                    nc.tensor.transpose(t[:, 2 * j + u, :], words[:, u::2], ident[:])
+            nc.scalar.copy(
+                out=wg[c][:, 1024 * a : 1024 * (a + 1)].bitcast(F32).rearrange("p (r s) -> p r s", s=4),
+                in_=t[:].rearrange("p s r -> p r s"),
+            )
+
+        def w_quant(c):
+            wc[c] = work.tile([P, CHUNK], U32, name="wc", tag="wc", bufs=2, align_bytes=64)
+            ws[c] = work.tile([P, CHUNK], U8, name="ws", tag="ws", bufs=2, align_bytes=64)
+            nc.vector.quantize_mx(out=wc[c][:].bitcast(FP8X4), scales=ws[c][:], in_=wg[c][:])
+
+        def bias10(c):
+            cols = slice(CHUNK * c, CHUNK * (c + 1))
+            nc.gpsimd.tensor_scalar(
+                out=cb10[:, cols], in0=cb[:, cols], scalar1=10.0, scalar2=0.0, op0=ALU.mult, op1=ALU.add
+            )
+
+        sps = {}
+        x = {}
+
+        def s_matmul(q, k):
+            c, j = divmod(q, 4)
+            i = 2 * j + k
+            rows = slice(P * i, P * (i + 1))
+            sps[q, k] = psum.tile([P, 512], F32, name="mm", tag="mm", bufs=5)
+            nc.tensor.matmul_mx(
+                out=sps[q, k][:],
+                lhsT=zc[:, rows].bitcast(FP8X4),
+                lhsT_scale=zs[:, rows],
+                rhs=wc[c][:].bitcast(FP8X4),
+                rhs_scale=ws[c][:],
+                start=True,
+                stop=True,
+            )
+
+        def s_bias(q, k):
+            c = q // 4
+            cols = slice(CHUNK * c, CHUNK * (c + 1))
+            if q not in x:
+                x[q] = work.tile([P, 2, CHUNK], F32, name="x", tag="x", bufs=4, align_bytes=64)
+            if (q, k) in SHIFT:
+                xs = work.tile([P, CHUNK], F32, name="xs", tag="xs", bufs=3, align_bytes=64)
+                nc.scalar.activation(out=xs[:], in_=sps[q, k][:], func=ACT.Copy, scale=10.0)
+                nc.gpsimd.tensor_tensor(out=x[q][:, k, :], in0=xs[:], in1=cb10[:, cols], op=ALU.add)
+            else:
+                nc.vector.scalar_tensor_tensor(
+                    out=x[q][:, k, :], in0=sps[q, k][:], scalar=10.0, in1=cb10[:, cols], op0=ALU.mult, op1=ALU.add
+                )
+
+        def s_min(q):
+            c, j = divmod(q, 4)
+            nc.vector.tensor_reduce(
+                out=mn[:, 2 * j : 2 * j + 2, MODS * c : MODS * (c + 1)],
+                in_=x[q][:].rearrange("p a (m k) -> p a m k", k=K),
+                axis=AX.X,
+                op=ALU.min,
+            )
+
+        def s_exp(q):
+            c, j = divmod(q, 4)
+            e = work.tile([P, 2, CHUNK], F32, name="e", tag="e", bufs=2, align_bytes=64)
+            for k in range(2):
+                for m in range(MODS):
+                    i = 2 * j + k
+                    mod = MODS * c + m
+                    nc.scalar.activation(
+                        out=e[:, k, K * m : K * (m + 1)],
+                        in_=x[q][:, k, K * m : K * (m + 1)],
+                        func=ACT.Exp,
+                        scale=-1.0,
+                        bias=mn[:, i, mod : mod + 1],
+                        accum_out=sums[:, i, mod : mod + 1],
+                    )
+
+        bias10(0)
+        for a in range(2):
+            for j in range(2):
+                if PROD[1] == "g":
+                    w_prod(1, a, j)
+        h_transpose(0)
+        h_transpose(1)
+        h_quant(0)
+        w_prod(0, 0, 0)
+        h_quant(1)
+        z_matmul(0)
+        z_matmul(1)
+        w_prod(0, 0, 1)
+        z_add(0)
+        w_transpose(0, 0)
+        h_transpose(2)
+        z_add(1)
+        w_prod(0, 1, 0)
+        z_round(0)
+        w_prod(0, 1, 1)
+        z_round(1)
+        z_transpose(0)
+        w_transpose(0, 1)
+        h_transpose(3)
+        h_quant(2)
+        z_quant(0)
+        w_quant(0)
+        h_quant(3)
+
+        npairs = 4 * NCH
+        for q in range(npairs + 1):
+            c, j = divmod(q, 4)
+            if q < npairs:
+                if c + 1 < NCH and j == 0:
+                    if c + 2 < NCH:
+                        bias10(c + 1)
+                        if PROD[c + 2] == "g":
+                            for a in range(2):
+                                for jj in range(2):
+                                    w_prod(c + 2, a, jj)
+                    elif c + 1 < NCH:
+                        bias10(c + 1)
+                s_matmul(q, 0)
+                s_matmul(q, 1)
+                if c == 0 and j < 3:
+                    z_matmul(2 * j + 2)
+                    z_matmul(2 * j + 3)
+                    if j < 2:
+                        h_transpose(2 * j + 4)
+                        h_transpose(2 * j + 5)
+                if c == 0 and j < 3:
+                    z_add(2 * j + 2)
+                for k in range(2):
+                    if (q, k) in SHIFT:
+                        s_bias(q, k)
+                if (q, 0) not in SHIFT:
+                    s_bias(q, 0)
+                if c == 0 and j < 3:
+                    z_add(2 * j + 3)
+                    z_round(2 * j + 2)
+            if q > 0:
+                s_min(q - 1)
+            if q < npairs:
+                if (q, 1) not in SHIFT:
+                    s_bias(q, 1)
+                if c == 0 and j < 3:
+                    z_round(2 * j + 3)
+                    z_transpose(j + 1)
+                    if j < 2:
+                        h_quant(2 * j + 4)
+                        h_quant(2 * j + 5)
+                    z_quant(j + 1)
+            if q > 0:
+                s_exp(q - 1)
+            if q < npairs and c + 1 < NCH:
+                if PROD[c + 1] in "vm":
+                    if j < 2:
+                        w_prod(c + 1, j, 0)
+                        w_prod(c + 1, j, 1)
+                if j in (1, 2):
+                    w_transpose(c + 1, j - 1)
+                if j == 3:
+                    w_quant(c + 1)
+
+        lns = keep.tile([P, BT, C], F32, name="lns", align_bytes=64)
+        conf = keep.tile([P, BT, C], F32, name="conf", align_bytes=64)
+        nc.scalar.activation(out=lns[:], in_=sums[:], func=ACT.Ln)
+        nc.vector.tensor_tensor(out=conf[:], in0=mn[:], in1=lns[:], op=ALU.subtract)
+        nc.sync.dma_start(out=out_conf.rearrange("(i p) c -> p i c", p=P), in_=conf[:])

@@ -26,6 +26,16 @@ ACT = mybir.ActivationFunctionType
 AX = mybir.AxisListType
 
 PROD = "vggggggg"
+WT = (1, 2)
+WQ = 3
+GQ = 2
+ZR = "ssssssss"
+WX = ()
+TG = 1
+PJ = 3
+GS = 1
+WA = 0
+WB = 0
 SHIFT = frozenset()
 
 
@@ -53,47 +63,44 @@ def tile_ace_pa_w4_kernel(tc, h_enc, w_words, w_scales, enc_b2, cw_bytes, cw_sca
         dummy = keep.tile([P, 8], F32, name="dummy")
         dummy2 = keep.tile([P, 8], F32, name="dummy2")
 
-        def load_h(i):
-            nc.sync.dma_start(out=h_in[:, i, :], in_=h_enc[P * i : P * (i + 1), :])
+        def load_h(i, e):
+            nc.sync.dma_start(out=h_in[:, i:e, :], in_=h_enc[P * i : P * e, :].rearrange("(i p) k -> p i k", p=P))
 
-        cw_rows = cw_bytes.rearrange("m h d -> (m h) d").rearrange("(c a r j) d -> c r a (j d)", a=2, r=P, j=2)
+        cw_rows = cw_bytes.rearrange("m h d -> (m h) d").rearrange("(c a r j) d -> r c a (j d)", a=2, r=P, j=2)
 
-        def load_w(c):
-            nc.sync.dma_start(out=cwb[:, c, :, :], in_=cw_rows[c])
+        def load_w(c, e):
+            nc.sync.dma_start(out=cwb[:, c:e, :, :], in_=cw_rows[:, c:e, :, :])
 
         cb_row = clus_b.rearrange("c k -> (c k)")
 
-        def load_cb(s, e):
-            nc.sync.dma_start(out=cb[:, s:e], in_=cb_row[s:e].partition_broadcast(P))
+        def load_cb(queue, s, e):
+            queue.dma_start(out=cb[:, s:e], in_=cb_row[s:e].partition_broadcast(P))
 
+        nc.gpsimd.dma_start(out=scale[:], in_=cw_scale.rearrange("a b d -> (a b d)").partition_broadcast(P))
         nc.gpsimd.memset(wqs[:].rearrange("p g n -> p (g n)").bitcast(I32), 0)
         nc.gpsimd.memset(dummy[:], 0.0)
         make_identity(nc, ident[:])
         nc.scalar.activation(out=dummy2[:], in_=dummy[:], func=ACT.Exp)
+        nc.gpsimd.dma_start(out=b2[:], in_=enc_b2.partition_broadcast(P))
+        load_cb(nc.gpsimd, 0, 512)
 
-        load_h(0)
-        load_h(1)
+        load_h(0, 1)
+        load_h(1, 2)
         nc.sync.dma_start(out=wq[:], in_=w_words.rearrange("g p x -> p g x"))
+        load_w(0, 1)
         for q in range(4):
             nc.sync.dma_start(
                 out=wqs[32 * q : 32 * q + 4, :, :].bitcast(I32),
                 in_=w_scales[:, 4 * q : 4 * q + 4, :].rearrange("g r n -> r g n").bitcast(I32),
             )
-        nc.sync.dma_start(out=scale[:], in_=cw_scale.rearrange("a b d -> (a b d)").partition_broadcast(P))
-        load_w(0)
-        load_h(2)
-        load_h(3)
-        nc.sync.dma_start(out=b2[:], in_=enc_b2.partition_broadcast(P))
-        load_cb(0, 512)
-        load_w(1)
-        for i in range(4, BT):
-            load_h(i)
-        load_cb(512, 2048)
-        load_w(2)
-        load_w(3)
-        load_cb(2048, 4096)
-        for c in range(4, NCH):
-            load_w(c)
+        load_h(2, 4)
+        load_h(4, 6)
+        load_h(6, 8)
+        load_w(1, 2)
+        load_cb(nc.sync, 512, 2048)
+        load_w(2, 4)
+        load_cb(nc.sync, 2048, 4096)
+        load_w(4, 8)
 
         def bank_tile(tag, bufs):
             t = psum.tile([P, 4, P], F32, name=tag, tag=tag, bufs=bufs)
@@ -116,15 +123,15 @@ def tile_ace_pa_w4_kernel(tc, h_enc, w_words, w_scales, enc_b2, cw_bytes, cw_sca
             for g in range(2):
                 for u in range(2):
                     nc.tensor.transpose(t[:, 2 * g + u, :], words[:, 256 * g + u : 256 * (g + 1) : 2], ident[:])
-            hg[i] = work.tile([P, 4 * 256], BF16, name="hg", tag="hg", bufs=3, align_bytes=64)
+            hg[i] = work.tile([P, 4 * 256], BF16, name="hg", tag="hg", bufs=8, align_bytes=64)
             nc.scalar.copy(
                 out=hg[i][:].bitcast(F32).rearrange("p (g b u) -> p g b u", g=2, u=2),
                 in_=t[:].rearrange("p (g u) b -> p g b u", u=2),
             )
 
         def h_quant(i):
-            hc[i] = work.tile([P, 256], U32, name="hc", tag="hc", bufs=4, align_bytes=64)
-            hs[i] = work.tile([P, 256], U8, name="hs", tag="hs", bufs=4, align_bytes=64)
+            hc[i] = work.tile([P, 256], U32, name="hc", tag="hc", bufs=8, align_bytes=64)
+            hs[i] = work.tile([P, 256], U8, name="hs", tag="hs", bufs=8, align_bytes=64)
             nc.vector.quantize_mx(out=hc[i][:].bitcast(FP8X4), scales=hs[i][:], in_=hg[i][:])
 
         zps = {}
@@ -143,24 +150,21 @@ def tile_ace_pa_w4_kernel(tc, h_enc, w_words, w_scales, enc_b2, cw_bytes, cw_sca
                 )
 
         def z_add(i):
-            zf[i] = work.tile([P, L], F32, name="zf", tag="zf", bufs=4, align_bytes=64)
+            zf[i] = work.tile([P, L], F32, name="zf", tag="zf", bufs=6, align_bytes=64)
             nc.vector.tensor_tensor(out=zf[i][:], in0=zps[i][:], in1=b2[:], op=ALU.add)
             nc.sync.dma_start(out=out_z[P * i : P * (i + 1), :], in_=zf[i][:])
 
-        def z_round(i):
-            zb[i] = work.tile([P, L], BF16, name="zb", tag="zb", bufs=4, align_bytes=64)
-            nc.vector.tensor_copy(out=zb[i][:], in_=zf[i][:])
-
-        def z_transpose(j):
+        def z_transpose(i):
             t = bank_tile("tr", 3)
-            for a in range(2):
-                words = zb[2 * j + a][:].bitcast(F32)
-                for u in range(2):
-                    nc.tensor.transpose(t[:, 2 * a + u, :], words[:, u::2], ident[:])
-            zg[j] = work.tile([P, 4 * 256], BF16, name="zg", tag="zg", bufs=2, align_bytes=64)
-            nc.scalar.copy(
-                out=zg[j][:].bitcast(F32).rearrange("p (a b u) -> p a b u", a=2, u=2),
-                in_=t[:].rearrange("p (a u) b -> p a b u", u=2),
+            for tt in range(4):
+                nc.tensor.transpose(t[:, tt, :], zf[i][:, tt::4], ident[:])
+            j, a = divmod(i, 2)
+            if a == 0:
+                zg[j] = work.tile([P, 2 * L], BF16, name="zg", tag="zg", bufs=4, align_bytes=64)
+            copy = nc.vector.tensor_copy if ZR[i] == "v" else nc.scalar.copy
+            copy(
+                out=zg[j][:, L * a : L * (a + 1)].rearrange("p (b t) -> p b t", t=4),
+                in_=t[:].rearrange("p t b -> p b t"),
             )
 
         def z_quant(j):
@@ -176,11 +180,10 @@ def tile_ace_pa_w4_kernel(tc, h_enc, w_words, w_scales, enc_b2, cw_bytes, cw_sca
                 nc.vector.tensor_tensor(out=dst, in0=src, in1=scale[:], op=ALU.mult)
             else:
                 wide = work.tile([P, L], BF16, name="wide", tag="wide", bufs=4, align_bytes=64)
-                if PROD[c] == "g":
-                    nc.gpsimd.tensor_copy(out=wide[:], in_=src)
-                elif PROD[c] == "m":
-                    nc.vector.tensor_copy(out=wide[:], in_=src)
-                nc.gpsimd.tensor_tensor(out=dst, in0=wide[:], in1=scale[:], op=ALU.mult)
+                for s in range(0, L, L // GS):
+                    e = s + L // GS
+                    nc.gpsimd.tensor_copy(out=wide[:, s:e], in_=src[:, s:e])
+                    nc.gpsimd.tensor_tensor(out=dst[:, s:e], in0=wide[:, s:e], in1=scale[:, s:e], op=ALU.mult)
 
         def w_transpose(c, a):
             if a == 0:
@@ -190,7 +193,8 @@ def tile_ace_pa_w4_kernel(tc, h_enc, w_words, w_scales, enc_b2, cw_bytes, cw_sca
                 words = prod[c, a][:, j, :].bitcast(F32)
                 for u in range(2):
                     nc.tensor.transpose(t[:, 2 * j + u, :], words[:, u::2], ident[:])
-            nc.scalar.copy(
+            copy = nc.vector.tensor_copy if (c > 0 and a in WX) else nc.scalar.copy
+            copy(
                 out=wg[c][:, 1024 * a : 1024 * (a + 1)].bitcast(F32).rearrange("p (r s) -> p r s", s=4),
                 in_=t[:].rearrange("p s r -> p r s"),
             )
@@ -209,13 +213,14 @@ def tile_ace_pa_w4_kernel(tc, h_enc, w_words, w_scales, enc_b2, cw_bytes, cw_sca
         sps = {}
         x = {}
 
-        def s_matmul(q, k):
-            c, j = divmod(q, 4)
-            i = 2 * j + k
+        nhalf = 8 * NCH
+
+        def s_matmul(n):
+            c, i = divmod(n, 8)
             rows = slice(P * i, P * (i + 1))
-            sps[q, k] = psum.tile([P, 512], F32, name="mm", tag="mm", bufs=5)
+            sps[n] = psum.tile([P, 512], F32, name="mm", tag="mm", bufs=5)
             nc.tensor.matmul_mx(
-                out=sps[q, k][:],
+                out=sps[n][:],
                 lhsT=zc[:, rows].bitcast(FP8X4),
                 lhsT_scale=zs[:, rows],
                 rhs=wc[c][:].bitcast(FP8X4),
@@ -224,131 +229,143 @@ def tile_ace_pa_w4_kernel(tc, h_enc, w_words, w_scales, enc_b2, cw_bytes, cw_sca
                 stop=True,
             )
 
-        def s_bias(q, k):
-            c = q // 4
+        groups = []
+        n0 = 0
+        while n0 < nhalf:
+            w = GQ if 8 <= n0 < nhalf - 8 else 2
+            groups.append((n0, w))
+            n0 += w
+        group_of = {}
+        for g, (n0, w) in enumerate(groups):
+            for k in range(w):
+                group_of[n0 + k] = (g, k)
+
+        def s_bias(n):
+            c = n // 8
             cols = slice(CHUNK * c, CHUNK * (c + 1))
-            if q not in x:
-                x[q] = work.tile([P, 2, CHUNK], F32, name="x", tag="x", bufs=4, align_bytes=64)
-            if (q, k) in SHIFT:
+            g, k = group_of[n]
+            if k == 0:
+                x[g] = work.tile([P, GQ, CHUNK], F32, name="x", tag="x", bufs=4, align_bytes=64)
+            if n in SHIFT:
                 xs = work.tile([P, CHUNK], F32, name="xs", tag="xs", bufs=3, align_bytes=64)
-                nc.scalar.activation(out=xs[:], in_=sps[q, k][:], func=ACT.Copy, scale=10.0)
-                nc.gpsimd.tensor_tensor(out=x[q][:, k, :], in0=xs[:], in1=cb10[:, cols], op=ALU.add)
+                nc.scalar.activation(out=xs[:], in_=sps[n][:], func=ACT.Copy, scale=10.0)
+                nc.gpsimd.tensor_tensor(out=x[g][:, k, :], in0=xs[:], in1=cb10[:, cols], op=ALU.add)
             else:
                 nc.vector.scalar_tensor_tensor(
-                    out=x[q][:, k, :], in0=sps[q, k][:], scalar=10.0, in1=cb10[:, cols], op0=ALU.mult, op1=ALU.add
+                    out=x[g][:, k, :], in0=sps[n][:], scalar=10.0, in1=cb10[:, cols], op0=ALU.mult, op1=ALU.add
                 )
 
-        def s_min(q):
-            c, j = divmod(q, 4)
+        def s_min(g):
+            n0, w = groups[g]
+            c, i = divmod(n0, 8)
             nc.vector.tensor_reduce(
-                out=mn[:, 2 * j : 2 * j + 2, MODS * c : MODS * (c + 1)],
-                in_=x[q][:].rearrange("p a (m k) -> p a m k", k=K),
+                out=mn[:, i : i + w, MODS * c : MODS * (c + 1)],
+                in_=x[g][:, :w, :].rearrange("p a (m k) -> p a m k", k=K),
                 axis=AX.X,
                 op=ALU.min,
             )
 
-        def s_exp(q):
-            c, j = divmod(q, 4)
-            e = work.tile([P, 2, CHUNK], F32, name="e", tag="e", bufs=2, align_bytes=64)
-            for k in range(2):
-                for m in range(MODS):
-                    i = 2 * j + k
-                    mod = MODS * c + m
-                    nc.scalar.activation(
-                        out=e[:, k, K * m : K * (m + 1)],
-                        in_=x[q][:, k, K * m : K * (m + 1)],
-                        func=ACT.Exp,
-                        scale=-1.0,
-                        bias=mn[:, i, mod : mod + 1],
-                        accum_out=sums[:, i, mod : mod + 1],
-                    )
+        def s_exp(n):
+            c, i = divmod(n, 8)
+            g, k = group_of[n]
+            e = work.tile([P, CHUNK], F32, name="e", tag="e", bufs=3, align_bytes=64)
+            for m in range(MODS):
+                mod = MODS * c + m
+                nc.scalar.activation(
+                    out=e[:, K * m : K * (m + 1)],
+                    in_=x[g][:, k, K * m : K * (m + 1)],
+                    func=ACT.Exp,
+                    scale=-1.0,
+                    bias=mn[:, i, mod : mod + 1],
+                    accum_out=sums[:, i, mod : mod + 1],
+                )
+
+        def w_prod_chunk(c):
+            for a in range(2):
+                for jj in range(2):
+                    w_prod(c, a, jj)
 
         bias10(0)
-        for a in range(2):
-            for j in range(2):
-                if PROD[1] == "g":
-                    w_prod(1, a, j)
         h_transpose(0)
         h_transpose(1)
         h_quant(0)
-        w_prod(0, 0, 0)
-        h_quant(1)
         z_matmul(0)
+        w_prod(0, 0, 0)
+        h_transpose(2)
+        h_quant(1)
         z_matmul(1)
         w_prod(0, 0, 1)
         z_add(0)
-        w_transpose(0, 0)
-        h_transpose(2)
-        z_add(1)
-        w_prod(0, 1, 0)
-        z_round(0)
-        w_prod(0, 1, 1)
-        z_round(1)
         z_transpose(0)
-        w_transpose(0, 1)
+        w_transpose(0, 0)
+        w_prod(0, 1, 0)
         h_transpose(3)
-        h_quant(2)
+        z_add(1)
+        z_transpose(1)
+        w_prod(0, 1, 1)
+        w_transpose(0, 1)
+        for i in (2, 3):
+            h_quant(i)
+            z_matmul(i)
+        if TG < 0 and PROD[1] == "g":
+            w_prod_chunk(1)
         z_quant(0)
         w_quant(0)
-        h_quant(3)
-
-        npairs = 4 * NCH
-        for q in range(npairs + 1):
-            c, j = divmod(q, 4)
-            if q < npairs:
-                if c + 1 < NCH and j == 0:
-                    if c + 2 < NCH:
-                        bias10(c + 1)
-                        if PROD[c + 2] == "g":
-                            for a in range(2):
-                                for jj in range(2):
-                                    w_prod(c + 2, a, jj)
-                    elif c + 1 < NCH:
-                        bias10(c + 1)
-                s_matmul(q, 0)
-                s_matmul(q, 1)
-                if c == 0 and j < 3:
-                    z_matmul(2 * j + 2)
-                    z_matmul(2 * j + 3)
-                    if j < 2:
-                        h_transpose(2 * j + 4)
-                        h_transpose(2 * j + 5)
-                if c == 0 and j < 3:
-                    z_add(2 * j + 2)
-                for k in range(2):
-                    if (q, k) in SHIFT:
-                        s_bias(q, k)
-                if (q, 0) not in SHIFT:
-                    s_bias(q, 0)
-                if c == 0 and j < 3:
-                    z_add(2 * j + 3)
-                    z_round(2 * j + 2)
-            if q > 0:
-                s_min(q - 1)
-            if q < npairs:
-                if (q, 1) not in SHIFT:
-                    s_bias(q, 1)
-                if c == 0 and j < 3:
-                    z_round(2 * j + 3)
-                    z_transpose(j + 1)
-                    if j < 2:
-                        h_quant(2 * j + 4)
-                        h_quant(2 * j + 5)
-                    z_quant(j + 1)
-            if q > 0:
-                s_exp(q - 1)
-            if q < npairs and c + 1 < NCH:
-                if PROD[c + 1] in "vm":
-                    if j < 2:
-                        w_prod(c + 1, j, 0)
-                        w_prod(c + 1, j, 1)
-                if j in (1, 2):
-                    w_transpose(c + 1, j - 1)
-                if j == 3:
-                    w_quant(c + 1)
+        for p in range(4 * NCH + 1):
+            c, j = divmod(p, 4)
+            last = p == 4 * NCH
+            if p == TG and PROD[1] == "g":
+                w_prod_chunk(1)
+            if j == 0 and c + 1 < NCH:
+                bias10(c + 1)
+            if j == (PJ if c == 0 else 0) and c + 2 < NCH and PROD[c + 2] == "g":
+                w_prod_chunk(c + 2)
+            if c + 1 < NCH and PROD[c + 1] == "v" and j < 2:
+                w_prod(c + 1, j, 0)
+                w_prod(c + 1, j, 1)
+            if c == 0 and j < 2:
+                h_transpose(2 * j + 4)
+                h_transpose(2 * j + 5)
+            if c == 0 and j < 3:
+                z_add(2 * j + 2)
+                z_add(2 * j + 3)
+            if not last:
+                s_matmul(2 * p)
+                s_matmul(2 * p + 1)
+            if c == 0 and j < 3:
+                z_transpose(2 * j + 2)
+                z_transpose(2 * j + 3)
+            if c + 1 < NCH and WA == 0 and j in WT:
+                w_transpose(c + 1, WT.index(j))
+            if not last:
+                s_bias(2 * p)
+            if p > 0:
+                s_min(p - 1)
+            if c + 1 < NCH and WB == 0 and j == WQ:
+                w_quant(c + 1)
+            if not last:
+                s_bias(2 * p + 1)
+            if p > 0:
+                s_exp(2 * p - 2)
+                if c + 1 < NCH and WA == 1 and j in WT:
+                    w_transpose(c + 1, WT.index(j))
+                s_exp(2 * p - 1)
+            if c == 0 and j < 2:
+                for i in (2 * j + 4, 2 * j + 5):
+                    h_quant(i)
+                    z_matmul(i)
+            if c == 0 and j < 3:
+                z_quant(j + 1)
+            if c + 1 < NCH and WA == 2 and j in WT:
+                w_transpose(c + 1, WT.index(j))
+            if c + 1 < NCH and WB == 1 and j == WQ:
+                w_quant(c + 1)
 
         lns = keep.tile([P, BT, C], F32, name="lns", align_bytes=64)
         conf = keep.tile([P, BT, C], F32, name="conf", align_bytes=64)
-        nc.scalar.activation(out=lns[:], in_=sums[:], func=ACT.Ln)
-        nc.vector.tensor_tensor(out=conf[:], in0=mn[:], in1=lns[:], op=ALU.subtract)
+        for lo, hi in ((0, C - MODS), (C - MODS, C)):
+            nc.scalar.activation(out=lns[:, :, lo:hi], in_=sums[:, :, lo:hi], func=ACT.Ln)
+            nc.vector.tensor_tensor(
+                out=conf[:, :, lo:hi], in0=mn[:, :, lo:hi], in1=lns[:, :, lo:hi], op=ALU.subtract
+            )
         nc.sync.dma_start(out=out_conf.rearrange("(i p) c -> p i c", p=P), in_=conf[:])

@@ -31,6 +31,10 @@ WQ = 3
 GQ = 2
 ZR = "ssssssss"
 WX = ()
+NE = 3
+STEP0 = "S0 S1 a0 a1 h0 h1 z0 z1 w0 w1 u0 n0 Q0 u1 q0 m0 q1 m1 N0 k0 e0 e1"
+STEP1 = "S0 S1 w0 w1 u0 n0 Q0 u1 e0 e1"
+PRO = "h0 h1 q0 m0 p0 q1 m1 p1 a0 h2 a1 w0 z0 p2 p3 q2 h3 z1 w1 q3 m3 m2"
 TG = 1
 PJ = 3
 GS = 1
@@ -245,7 +249,7 @@ def tile_ace_pa_w4_kernel(tc, h_enc, w_words, w_scales, enc_b2, cw_bytes, cw_sca
             cols = slice(CHUNK * c, CHUNK * (c + 1))
             g, k = group_of[n]
             if k == 0:
-                x[g] = work.tile([P, GQ, CHUNK], F32, name="x", tag="x", bufs=4, align_bytes=64)
+                x[g] = work.tile([P, GQ, CHUNK], F32, name="x", tag="x", bufs=6, align_bytes=64)
             if n in SHIFT:
                 xs = work.tile([P, CHUNK], F32, name="xs", tag="xs", bufs=3, align_bytes=64)
                 nc.scalar.activation(out=xs[:], in_=sps[n][:], func=ACT.Copy, scale=10.0)
@@ -286,80 +290,69 @@ def tile_ace_pa_w4_kernel(tc, h_enc, w_words, w_scales, enc_b2, cw_bytes, cw_sca
                     w_prod(c, a, jj)
 
         bias10(0)
-        h_transpose(0)
-        h_transpose(1)
-        h_quant(0)
-        z_matmul(0)
-        w_prod(0, 0, 0)
-        h_transpose(2)
-        h_quant(1)
-        z_matmul(1)
-        w_prod(0, 0, 1)
-        z_add(0)
-        z_transpose(0)
-        w_transpose(0, 0)
-        w_prod(0, 1, 0)
-        h_transpose(3)
-        z_add(1)
-        z_transpose(1)
-        w_prod(0, 1, 1)
-        w_transpose(0, 1)
-        for i in (2, 3):
-            h_quant(i)
-            z_matmul(i)
+        pro = {
+            "h": lambda i: h_transpose(i),
+            "q": lambda i: h_quant(i),
+            "m": lambda i: z_matmul(i),
+            "p": lambda i: w_prod(0, i // 2, i % 2),
+            "a": lambda i: z_add(i),
+            "z": lambda i: z_transpose(i),
+            "w": lambda i: w_transpose(0, i),
+        }
+        for item in PRO.split():
+            pro[item[0]](int(item[1]))
         if TG < 0 and PROD[1] == "g":
             w_prod_chunk(1)
         z_quant(0)
         w_quant(0)
-        for p in range(4 * NCH + 1):
+        ready = []
+        pending = list(range(4 * NCH))
+        for p in range(4 * NCH + 3):
             c, j = divmod(p, 4)
-            last = p == 4 * NCH
+            last = p >= 4 * NCH
             if p == TG and PROD[1] == "g":
                 w_prod_chunk(1)
             if j == 0 and c + 1 < NCH:
                 bias10(c + 1)
             if j == (PJ if c == 0 else 0) and c + 2 < NCH and PROD[c + 2] == "g":
                 w_prod_chunk(c + 2)
-            if c + 1 < NCH and PROD[c + 1] == "v" and j < 2:
-                w_prod(c + 1, j, 0)
-                w_prod(c + 1, j, 1)
-            if c == 0 and j < 2:
-                h_transpose(2 * j + 4)
-                h_transpose(2 * j + 5)
-            if c == 0 and j < 3:
-                z_add(2 * j + 2)
-                z_add(2 * j + 3)
-            if not last:
-                s_matmul(2 * p)
-                s_matmul(2 * p + 1)
-            if c == 0 and j < 3:
-                z_transpose(2 * j + 2)
-                z_transpose(2 * j + 3)
-            if c + 1 < NCH and WA == 0 and j in WT:
-                w_transpose(c + 1, WT.index(j))
-            if not last:
-                s_bias(2 * p)
-            if p > 0:
-                s_min(p - 1)
-            if c + 1 < NCH and WB == 0 and j == WQ:
-                w_quant(c + 1)
-            if not last:
-                s_bias(2 * p + 1)
-            if p > 0:
-                s_exp(2 * p - 2)
-                if c + 1 < NCH and WA == 1 and j in WT:
-                    w_transpose(c + 1, WT.index(j))
-                s_exp(2 * p - 1)
-            if c == 0 and j < 2:
-                for i in (2 * j + 4, 2 * j + 5):
-                    h_quant(i)
-                    z_matmul(i)
-            if c == 0 and j < 3:
-                z_quant(j + 1)
-            if c + 1 < NCH and WA == 2 and j in WT:
-                w_transpose(c + 1, WT.index(j))
-            if c + 1 < NCH and WB == 1 and j == WQ:
-                w_quant(c + 1)
+            for item in (STEP0 if c == 0 else STEP1).split():
+                k = item[0]
+                v = int(item[1])
+                if k == "a" and c == 0 and j < 3:
+                    z_add(2 * j + 2 + v)
+                if k == "S" and not last:
+                    s_matmul(2 * p + v)
+                if k == "h" and c == 0 and j < 2:
+                    h_transpose(2 * j + 4 + v)
+                if k == "z" and c == 0 and j < 3:
+                    z_transpose(2 * j + 2 + v)
+                if k == "w" and c + 1 < NCH and j == WT[v]:
+                    w_transpose(c + 1, v)
+                if k == "u" and not last:
+                    s_bias(2 * p + v)
+                if k == "n":
+                    while pending and pending[0] + (2 if 2 * pending[0] + 1 in SHIFT or 2 * pending[0] in SHIFT else 1) <= p:
+                        g = pending.pop(0)
+                        s_min(g)
+                        ready.extend([2 * g, 2 * g + 1])
+                if k == "N" and p < NE:
+                    g = pending.pop(0)
+                    assert g == p
+                    s_min(g)
+                    ready.extend([2 * g, 2 * g + 1])
+                if k == "e" and ready:
+                    s_exp(ready.pop(0))
+                if k == "q" and c == 0 and j < 2:
+                    h_quant(2 * j + 4 + v)
+                if k == "m" and c == 0 and j < 2:
+                    z_matmul(2 * j + 4 + v)
+                if k == "k" and c == 0 and j < 3:
+                    z_quant(j + 1)
+                if k == "Q" and c + 1 < NCH and j == WQ:
+                    w_quant(c + 1)
+
+        assert not ready and not pending
 
         lns = keep.tile([P, BT, C], F32, name="lns", align_bytes=64)
         conf = keep.tile([P, BT, C], F32, name="conf", align_bytes=64)

from contextlib import ExitStack

import concourse.mybir as mybir
from concourse.masks import make_identity

B, DIN, L, C, K = 1024, 1024, 512, 64, 64
FLOPS = 2 * B * DIN * L + 2 * B * L * C * K

P = 128
BT = B // P
CK = C * K
CHUNK = 512
NCH = CK // CHUNK
MODS = CHUNK // K

F32 = mybir.dt.float32
BF16 = mybir.dt.bfloat16
U32 = mybir.dt.uint32
I32 = mybir.dt.int32
U8 = mybir.dt.uint8
E4 = mybir.dt.float8_e4m3fn
FP8X4 = mybir.dt.float8_e4m3fn_x4
FP4X4 = mybir.dt.float4_e2m1fn_x4
ALU = mybir.AluOpType
ACT = mybir.ActivationFunctionType
AX = mybir.AxisListType

PROD = "vggggggg"
WT = (1, 2)
WQ = 3
GQ = 2
ZR = "ssssssss"
WX = ()
NE = 3
STEP0 = "S0 S1 a0 a1 h0 h1 z0 z1 w0 w1 u0 n0 Q0 u1 q0 m0 q1 m1 N0 k0 e0 e1"
STEP1 = "S0 S1 w0 w1 u0 n0 Q0 u1 e0 e1"
PRO = "h0 h1 q0 m0 p0 q1 m1 p1 a0 h2 a1 w0 z0 p2 p3 q2 h3 z1 w1 q3 m3 m2"
TG = 1
PJ = 3
GS = 1
WA = 0
WB = 0
SHIFT = frozenset()


def tile_ace_pa_w4_kernel(tc, h_enc, w_words, w_scales, enc_b2, cw_bytes, cw_scale, clus_b, out_z, out_conf):
    nc = tc.nc
    with ExitStack() as ctx:
        keep = ctx.enter_context(tc.tile_pool(name="keep", bufs=1))
        work = ctx.enter_context(tc.tile_pool(name="work", bufs=3))
        psum = ctx.enter_context(tc.psum_pool(name="psum", bufs=1))
        ctx.enter_context(tc.manual_schedule())

        ident = keep.tile([P, P], F32, name="ident")
        h_in = keep.tile([P, BT, DIN], BF16, name="h_in", align_bytes=64)
        wq = keep.tile([P, 2, 2 * L], U8, name="wq", align_bytes=64)
        wqs = keep.tile([P, 2, L], U8, name="wqs", align_bytes=64)
        b2 = keep.tile([P, L], BF16, name="b2", align_bytes=64)
        scale = keep.tile([P, L], F32, name="scale", align_bytes=64)
        cwb = keep.tile([P, NCH, 2, 2 * L], U8, name="cwb", align_bytes=64)
        cb = keep.tile([P, CK], BF16, name="cb", align_bytes=64)
        cb10 = keep.tile([P, CK], F32, name="cb10", align_bytes=64)
        zc = keep.tile([P, B], U32, name="zc", align_bytes=64)
        zs = keep.tile([P, B], U8, name="zs", align_bytes=64)
        mn = keep.tile([P, BT, C], F32, name="mn", align_bytes=64)
        sums = keep.tile([P, BT, C], F32, name="sums", align_bytes=64)
        dummy = keep.tile([P, 8], F32, name="dummy")
        dummy2 = keep.tile([P, 8], F32, name="dummy2")

        def load_h(i, e):
            nc.sync.dma_start(out=h_in[:, i:e, :], in_=h_enc[P * i : P * e, :].rearrange("(i p) k -> p i k", p=P))

        cw_rows = cw_bytes.rearrange("m h d -> (m h) d").rearrange("(c a r j) d -> r c a (j d)", a=2, r=P, j=2)

        def load_w(c, e):
            nc.sync.dma_start(out=cwb[:, c:e, :, :], in_=cw_rows[:, c:e, :, :])

        cb_row = clus_b.rearrange("c k -> (c k)")

        def load_cb(queue, s, e):
            queue.dma_start(out=cb[:, s:e], in_=cb_row[s:e].partition_broadcast(P))

        nc.gpsimd.dma_start(out=scale[:], in_=cw_scale.rearrange("a b d -> (a b d)").partition_broadcast(P))
        nc.gpsimd.memset(wqs[:].rearrange("p g n -> p (g n)").bitcast(I32), 0)
        nc.gpsimd.memset(dummy[:], 0.0)
        make_identity(nc, ident[:])
        nc.scalar.activation(out=dummy2[:], in_=dummy[:], func=ACT.Exp)
        nc.gpsimd.dma_start(out=b2[:], in_=enc_b2.partition_broadcast(P))
        load_cb(nc.gpsimd, 0, 512)

        load_h(0, 1)
        load_h(1, 2)
        nc.sync.dma_start(out=wq[:], in_=w_words.rearrange("g p x -> p g x"))
        load_w(0, 1)
        for q in range(4):
            nc.sync.dma_start(
                out=wqs[32 * q : 32 * q + 4, :, :].bitcast(I32),
                in_=w_scales[:, 4 * q : 4 * q + 4, :].rearrange("g r n -> r g n").bitcast(I32),
            )
        load_h(2, 4)
        load_h(4, 6)
        load_h(6, 8)
        load_w(1, 2)
        load_cb(nc.sync, 512, 2048)
        load_w(2, 4)
        load_cb(nc.sync, 2048, 4096)
        load_w(4, 8)

        def bank_tile(tag, bufs):
            t = psum.tile([P, 4, P], F32, name=tag, tag=tag, bufs=bufs)
            return t

        hg = {}
        hc = {}
        hs = {}
        zf = {}
        zb = {}
        zg = {}
        prod = {}
        wg = {}
        wc = {}
        ws = {}

        def h_transpose(i):
            words = h_in[:, i, :].bitcast(F32)
            t = bank_tile("tr", 3)
            for g in range(2):
                for u in range(2):
                    nc.tensor.transpose(t[:, 2 * g + u, :], words[:, 256 * g + u : 256 * (g + 1) : 2], ident[:])
            hg[i] = work.tile([P, 4 * 256], BF16, name="hg", tag="hg", bufs=8, align_bytes=64)
            nc.scalar.copy(
                out=hg[i][:].bitcast(F32).rearrange("p (g b u) -> p g b u", g=2, u=2),
                in_=t[:].rearrange("p (g u) b -> p g b u", u=2),
            )

        def h_quant(i):
            hc[i] = work.tile([P, 256], U32, name="hc", tag="hc", bufs=8, align_bytes=64)
            hs[i] = work.tile([P, 256], U8, name="hs", tag="hs", bufs=8, align_bytes=64)
            nc.vector.quantize_mx(out=hc[i][:].bitcast(FP8X4), scales=hs[i][:], in_=hg[i][:])

        zps = {}

        def z_matmul(i):
            zps[i] = psum.tile([P, 512], F32, name="mm", tag="mm", bufs=5)
            for g in range(2):
                nc.tensor.matmul_mx(
                    out=zps[i][:],
                    lhsT=hc[i][:, P * g : P * (g + 1)].bitcast(FP8X4),
                    lhsT_scale=hs[i][:, P * g : P * (g + 1)],
                    rhs=wq[:, g, :].bitcast(FP4X4),
                    rhs_scale=wqs[:, g, :],
                    start=(g == 0),
                    stop=(g == 1),
                )

        def z_add(i):
            zf[i] = work.tile([P, L], F32, name="zf", tag="zf", bufs=6, align_bytes=64)
            nc.vector.tensor_tensor(out=zf[i][:], in0=zps[i][:], in1=b2[:], op=ALU.add)
            nc.sync.dma_start(out=out_z[P * i : P * (i + 1), :], in_=zf[i][:])

        def z_transpose(i):
            t = bank_tile("tr", 3)
            for tt in range(4):
                nc.tensor.transpose(t[:, tt, :], zf[i][:, tt::4], ident[:])
            j, a = divmod(i, 2)
            if a == 0:
                zg[j] = work.tile([P, 2 * L], BF16, name="zg", tag="zg", bufs=4, align_bytes=64)
            copy = nc.vector.tensor_copy if ZR[i] == "v" else nc.scalar.copy
            copy(
                out=zg[j][:, L * a : L * (a + 1)].rearrange("p (b t) -> p b t", t=4),
                in_=t[:].rearrange("p t b -> p b t"),
            )

        def z_quant(j):
            cols = slice(256 * j, 256 * (j + 1))
            nc.vector.quantize_mx(out=zc[:, cols].bitcast(FP8X4), scales=zs[:, cols], in_=zg[j][:])

        def w_prod(c, a, j):
            if j == 0:
                prod[c, a] = work.tile([P, 2, L], BF16, name="prod", tag="prod", bufs=6, align_bytes=64)
            src = cwb[:, c, a, L * j : L * (j + 1)].bitcast(E4)
            dst = prod[c, a][:, j, :]
            if PROD[c] == "v":
                nc.vector.tensor_tensor(out=dst, in0=src, in1=scale[:], op=ALU.mult)
            else:
                wide = work.tile([P, L], BF16, name="wide", tag="wide", bufs=4, align_bytes=64)
                for s in range(0, L, L // GS):
                    e = s + L // GS
                    nc.gpsimd.tensor_copy(out=wide[:, s:e], in_=src[:, s:e])
                    nc.gpsimd.tensor_tensor(out=dst[:, s:e], in0=wide[:, s:e], in1=scale[:, s:e], op=ALU.mult)

        def w_transpose(c, a):
            if a == 0:
                wg[c] = work.tile([P, 4 * CHUNK], BF16, name="wg", tag="wg", bufs=2, align_bytes=64)
            t = bank_tile("tr", 3)
            for j in range(2):
                words = prod[c, a][:, j, :].bitcast(F32)
                for u in range(2):
                    nc.tensor.transpose(t[:, 2 * j + u, :], words[:, u::2], ident[:])
            copy = nc.vector.tensor_copy if (c > 0 and a in WX) else nc.scalar.copy
            copy(
                out=wg[c][:, 1024 * a : 1024 * (a + 1)].bitcast(F32).rearrange("p (r s) -> p r s", s=4),
                in_=t[:].rearrange("p s r -> p r s"),
            )

        def w_quant(c):
            wc[c] = work.tile([P, CHUNK], U32, name="wc", tag="wc", bufs=2, align_bytes=64)
            ws[c] = work.tile([P, CHUNK], U8, name="ws", tag="ws", bufs=2, align_bytes=64)
            nc.vector.quantize_mx(out=wc[c][:].bitcast(FP8X4), scales=ws[c][:], in_=wg[c][:])

        def bias10(c):
            cols = slice(CHUNK * c, CHUNK * (c + 1))
            nc.gpsimd.tensor_scalar(
                out=cb10[:, cols], in0=cb[:, cols], scalar1=10.0, scalar2=0.0, op0=ALU.mult, op1=ALU.add
            )

        sps = {}
        x = {}

        nhalf = 8 * NCH

        def s_matmul(n):
            c, i = divmod(n, 8)
            rows = slice(P * i, P * (i + 1))
            sps[n] = psum.tile([P, 512], F32, name="mm", tag="mm", bufs=5)
            nc.tensor.matmul_mx(
                out=sps[n][:],
                lhsT=zc[:, rows].bitcast(FP8X4),
                lhsT_scale=zs[:, rows],
                rhs=wc[c][:].bitcast(FP8X4),
                rhs_scale=ws[c][:],
                start=True,
                stop=True,
            )

        groups = []
        n0 = 0
        while n0 < nhalf:
            w = GQ if 8 <= n0 < nhalf - 8 else 2
            groups.append((n0, w))
            n0 += w
        group_of = {}
        for g, (n0, w) in enumerate(groups):
            for k in range(w):
                group_of[n0 + k] = (g, k)

        def s_bias(n):
            c = n // 8
            cols = slice(CHUNK * c, CHUNK * (c + 1))
            g, k = group_of[n]
            if k == 0:
                x[g] = work.tile([P, GQ, CHUNK], F32, name="x", tag="x", bufs=6, align_bytes=64)
            if n in SHIFT:
                xs = work.tile([P, CHUNK], F32, name="xs", tag="xs", bufs=3, align_bytes=64)
                nc.scalar.activation(out=xs[:], in_=sps[n][:], func=ACT.Copy, scale=10.0)
                nc.gpsimd.tensor_tensor(out=x[g][:, k, :], in0=xs[:], in1=cb10[:, cols], op=ALU.add)
            else:
                nc.vector.scalar_tensor_tensor(
                    out=x[g][:, k, :], in0=sps[n][:], scalar=10.0, in1=cb10[:, cols], op0=ALU.mult, op1=ALU.add
                )

        def s_min(g):
            n0, w = groups[g]
            c, i = divmod(n0, 8)
            nc.vector.tensor_reduce(
                out=mn[:, i : i + w, MODS * c : MODS * (c + 1)],
                in_=x[g][:, :w, :].rearrange("p a (m k) -> p a m k", k=K),
                axis=AX.X,
                op=ALU.min,
            )

        def s_exp(n):
            c, i = divmod(n, 8)
            g, k = group_of[n]
            e = work.tile([P, CHUNK], F32, name="e", tag="e", bufs=3, align_bytes=64)
            for m in range(MODS):
                mod = MODS * c + m
                nc.scalar.activation(
                    out=e[:, K * m : K * (m + 1)],
                    in_=x[g][:, k, K * m : K * (m + 1)],
                    func=ACT.Exp,
                    scale=-1.0,
                    bias=mn[:, i, mod : mod + 1],
                    accum_out=sums[:, i, mod : mod + 1],
                )

        def w_prod_chunk(c):
            for a in range(2):
                for jj in range(2):
                    w_prod(c, a, jj)

        bias10(0)
        pro = {
            "h": lambda i: h_transpose(i),
            "q": lambda i: h_quant(i),
            "m": lambda i: z_matmul(i),
            "p": lambda i: w_prod(0, i // 2, i % 2),
            "a": lambda i: z_add(i),
            "z": lambda i: z_transpose(i),
            "w": lambda i: w_transpose(0, i),
        }
        for item in PRO.split():
            pro[item[0]](int(item[1]))
        if TG < 0 and PROD[1] == "g":
            w_prod_chunk(1)
        z_quant(0)
        w_quant(0)
        ready = []
        pending = list(range(4 * NCH))
        for p in range(4 * NCH + 3):
            c, j = divmod(p, 4)
            last = p >= 4 * NCH
            if p == TG and PROD[1] == "g":
                w_prod_chunk(1)
            if j == 0 and c + 1 < NCH:
                bias10(c + 1)
            if j == (PJ if c == 0 else 0) and c + 2 < NCH and PROD[c + 2] == "g":
                w_prod_chunk(c + 2)
            for item in (STEP0 if c == 0 else STEP1).split():
                k = item[0]
                v = int(item[1])
                if k == "a" and c == 0 and j < 3:
                    z_add(2 * j + 2 + v)
                if k == "S" and not last:
                    s_matmul(2 * p + v)
                if k == "h" and c == 0 and j < 2:
                    h_transpose(2 * j + 4 + v)
                if k == "z" and c == 0 and j < 3:
                    z_transpose(2 * j + 2 + v)
                if k == "w" and c + 1 < NCH and j == WT[v]:
                    w_transpose(c + 1, v)
                if k == "u" and not last:
                    s_bias(2 * p + v)
                if k == "n":
                    while pending and pending[0] + (2 if 2 * pending[0] + 1 in SHIFT or 2 * pending[0] in SHIFT else 1) <= p:
                        g = pending.pop(0)
                        s_min(g)
                        ready.extend([2 * g, 2 * g + 1])
                if k == "N" and p < NE:
                    g = pending.pop(0)
                    assert g == p
                    s_min(g)
                    ready.extend([2 * g, 2 * g + 1])
                if k == "e" and ready:
                    s_exp(ready.pop(0))
                if k == "q" and c == 0 and j < 2:
                    h_quant(2 * j + 4 + v)
                if k == "m" and c == 0 and j < 2:
                    z_matmul(2 * j + 4 + v)
                if k == "k" and c == 0 and j < 3:
                    z_quant(j + 1)
                if k == "Q" and c + 1 < NCH and j == WQ:
                    w_quant(c + 1)

        assert not ready and not pending

        lns = keep.tile([P, BT, C], F32, name="lns", align_bytes=64)
        conf = keep.tile([P, BT, C], F32, name="conf", align_bytes=64)
        for lo, hi in ((0, C - MODS), (C - MODS, C)):
            nc.scalar.activation(out=lns[:, :, lo:hi], in_=sums[:, :, lo:hi], func=ACT.Ln)
            nc.vector.tensor_tensor(
                out=conf[:, :, lo:hi], in0=mn[:, :, lo:hi], in1=lns[:, :, lo:hi], op=ALU.subtract
            )
        nc.sync.dma_start(out=out_conf.rearrange("(i p) c -> p i c", p=P), in_=conf[:])
